import numpy as np
import ml_dtypes


def mxq(x, axis, fmt="e4m3"):
    dtype, down = {"e4m3": (ml_dtypes.float8_e4m3fn, 7), "e5m2": (ml_dtypes.float8_e5m2, 14)}[fmt]
    v = np.moveaxis(np.asarray(x, np.float32).astype(ml_dtypes.bfloat16).astype(np.float64), axis, -1)
    blocks = v.reshape(v.shape[:-1] + (-1, 32))
    amax = np.abs(blocks).max(-1, keepdims=True)
    byte = np.maximum(np.where(amax > 0, np.frexp(amax)[1] - 1 + 127, 0) - down, 1)
    scale = np.exp2(byte - 127.0)
    codes = (blocks / scale).astype(np.float32).astype(dtype).astype(np.float64)
    return np.moveaxis((codes * scale).reshape(v.shape), -1, axis)


WIDE = False


def mx_kscale(k):
    if not WIDE:
        return np.ones(k)
    levels = np.array([20, -20, 10, -10, 0])
    if k % 512:
        return np.exp2(np.random.permutation(np.resize(levels, k // 32))).repeat(32)
    a = np.empty((k // 512, 16))
    for p in range(k // 512):
        a[p, :8] = np.random.permutation(np.resize(levels, 8))
        for g in range(8):
            far = levels[np.abs(levels - a[p, g]) >= 10]
            a[p, g + 8] = far[np.random.randint(len(far))]
    return np.exp2(a.ravel()).repeat(32)


BF16 = ml_dtypes.bfloat16


def bf(x):
    return np.asarray(x, np.float32).astype(BF16)


def f64(x):
    return np.asarray(x).astype(np.float64)


B, NH, T, D, N = 1, 1, 128, 512, 1024
THETA = 2.0 ** 16
SCALE = N ** -0.5


def rope_tables():
    pair = np.repeat(np.arange(N // 2), 2)
    freqs = 1.0 / THETA ** (pair * 2.0 / N)
    angles = np.arange(T)[:, None] * freqs[None, :]
    return np.cos(angles), np.sin(angles)


def rope(v, cos, sin):
    v_rot = np.stack([-v[..., 1::2], v[..., ::2]], axis=-1).reshape(v.shape)
    return v * cos + v_rot * sin


def rope_adjoint(h, cos, sin):
    hs = h * sin
    hs_rot = np.stack([hs[..., 1::2], -hs[..., ::2]], axis=-1).reshape(h.shape)
    return h * cos + hs_rot


def setup_inputs():
    u = mx_kscale(D)
    cos, sin = rope_tables()
    Q = np.random.uniform(size=(B, NH, T, N)) * 1.2 / N ** 0.25
    V = np.random.standard_normal((B, 1, T, D)) * 45.0 / np.sqrt(T) / u
    state = np.random.standard_normal((B, NH, N, D)) * 60.0 / N ** 0.75 / u
    g = np.random.standard_normal((B, NH, N, D)) * np.exp2(np.random.randint(-12, 1, (B, NH, N, 1))) * 32.0 * u
    return {"Q": bf(Q), "V": bf(V), "state": bf(state), "cos": bf(cos), "sin": bf(sin), "grad_out": bf(g)}


def reference(Q, V, state, cos, sin, grad_out):
    gQR = (mxq(f64(V), 3, "e4m3") @ np.swapaxes(mxq(f64(grad_out), 3, "e5m2"), -2, -1)) * SCALE
    return rope_adjoint(gQR, f64(cos), f64(sin))

@@ -1,0 +1,160 @@
+import concourse.mybir as mybir
+from concourse.masks import make_identity
+
+F32 = mybir.dt.float32
+BF16 = mybir.dt.bfloat16
+U32 = mybir.dt.uint32
+U8 = mybir.dt.uint8
+E4M3_X4 = mybir.dt.float8_e4m3fn_x4
+E5M2_X4 = mybir.dt.float8_e5m2_x4
+MULT = mybir.AluOpType.mult
+ADD = mybir.AluOpType.add
+
+P = 128
+PACK = 4
+T = 128
+D = 512
+N = 1024
+SCALE = N ** -0.5
+
+HALVES = D // 2 // P
+PARITIES = 2
+CHUNK = P * PARITIES
+BANK = 512
+N_BANKS = N // BANK
+CHUNKS = BANK // CHUNK
+TURN_BANKS = 8 - N_BANKS
+
+FLOPS = 2 * T * N * D
+BYTES = 2 * (T * D + N * D + 2 * T * N) + 4 * T * N
+
+
+def transpose_rows(nc, psum, rows, ident):
+    words = rows.bitcast(F32)
+    turned = psum.tile([P, HALVES, P], F32, tag="turned")
+    for u in range(HALVES):
+        nc.tensor.transpose(turned[:, u, :], words[:, u :: HALVES], ident)
+    return turned
+
+
+def group_words(copy, grouped, turned):
+    copy(out=grouped.bitcast(F32), in_=turned[:].rearrange("p u r -> p r u"))
+
+
+def tile_attention_pb_s_kernel(tc, Q, V, state, cos, sin, grad_out, out):
+    nc = tc.nc
+    v_dram = V.flatten_outer_dims()
+    out_dram = out.flatten_outer_dims()
+    g_dram = grad_out.flatten_outer_dims().rearrange("(c p e) d -> c p e d", p=P, e=PARITIES)
+
+    with (
+        tc.tile_pool(name="keep", bufs=1) as keep,
+        tc.tile_pool(name="banks", bufs=N_BANKS) as banks,
+        tc.tile_pool(name="chunks", bufs=N_BANKS * CHUNKS) as chunks,
+        tc.tile_pool(name="planes", bufs=N_BANKS * CHUNKS * PARITIES) as planes,
+        tc.psum_pool(name="psum_turn", bufs=TURN_BANKS) as psum_turn,
+        tc.psum_pool(name="psum_h", bufs=N_BANKS) as psum_h,
+        tc.manual_schedule(),
+    ):
+        ident = keep.tile([P, P], F32)
+        make_identity(nc, ident[:])
+
+        v_rows = keep.tile([T, D], BF16)
+        nc.sync.dma_start(out=v_rows[:], in_=v_dram)
+        g_chunks = []
+        for c in range(N_BANKS * CHUNKS):
+            g_rows = chunks.tile([P, PARITIES, D], BF16)
+            nc.sync.dma_start(out=g_rows[:], in_=g_dram[c])
+            g_chunks.append(g_rows)
+        sin_banks = []
+        cos_banks = []
+        for b in range(N_BANKS):
+            cols = slice(b * BANK, (b + 1) * BANK)
+            sin_sb = banks.tile([T, BANK], BF16)
+            nc.sync.dma_start(out=sin_sb[:], in_=sin[:, cols])
+            sin_banks.append(sin_sb)
+            cos_sb = banks.tile([T, BANK], BF16)
+            nc.sync.dma_start(out=cos_sb[:], in_=cos[:, cols])
+            cos_banks.append(cos_sb)
+
+        v_grouped = keep.tile([P, T, PACK], BF16, align_bytes=64)
+        v_codes = keep.tile([P, T], U32, align_bytes=64)
+        v_scales = keep.tile([P, T], U8, align_bytes=64)
+        v_turned = transpose_rows(nc, psum_turn, v_rows[:], ident[:])
+        group_words(nc.vector.tensor_copy, v_grouped[:], v_turned)
+        nc.vector.quantize_mx(
+            out=v_codes[:].bitcast(E4M3_X4),
+            scales=v_scales[:],
+            in_=v_grouped[:].rearrange("p r t -> p (r t)"),
+        )
+
+        code_banks = []
+        scale_banks = []
+        for b in range(N_BANKS):
+            g_codes = banks.tile([P, CHUNKS, PARITIES, P], U32, align_bytes=64)
+            g_scales = banks.tile([P, CHUNKS, PARITIES, P], U8, align_bytes=64)
+            for c in range(CHUNKS):
+                for e in range(PARITIES):
+                    g_turned = transpose_rows(nc, psum_turn, g_chunks[b * CHUNKS + c][:, e, :], ident[:])
+                    g_grouped = planes.tile([P, P, PACK], BF16, align_bytes=64)
+                    group_words(nc.scalar.copy, g_grouped[:], g_turned)
+                    nc.vector.quantize_mx(
+                        out=g_codes[:, c, e, :].bitcast(E5M2_X4),
+                        scales=g_scales[:, c, e, :],
+                        in_=g_grouped[:].rearrange("p r t -> p (r t)"),
+                    )
+            code_banks.append(g_codes)
+            scale_banks.append(g_scales)
+
+        for b in range(N_BANKS):
+            h = psum_h.tile([T, BANK], F32)
+            nc.tensor.matmul_mx(
+                out=h[:],
+                lhsT=v_codes[:].bitcast(E4M3_X4),
+                lhsT_scale=v_scales[:],
+                rhs=code_banks[b][:].rearrange("p c e r -> p (c e r)").bitcast(E5M2_X4),
+                rhs_scale=scale_banks[b][:].rearrange("p c e r -> p (c e r)"),
+                start=True,
+                stop=True,
+            )
+
+            crossed = banks.tile([T, PARITIES, CHUNKS, P], F32)
+            h_by_parity = h[:].rearrange("t (c e p) -> t e c p", c=CHUNKS, e=PARITIES)
+            sin_by_parity = sin_banks[b][:].rearrange("t (c p e) -> t e c p", c=CHUNKS, e=PARITIES)
+            for e in range(PARITIES):
+                partner = 1 - e
+                nc.vector.scalar_tensor_tensor(
+                    out=crossed[:, e, :, :],
+                    in0=h_by_parity[:, partner],
+                    scalar=SCALE if e == 0 else -SCALE,
+                    in1=sin_by_parity[:, partner],
+                    op0=MULT,
+                    op1=MULT,
+                )
+            directs = []
+            for c in range(CHUNKS):
+                cols = slice(c * CHUNK, (c + 1) * CHUNK)
+                direct = chunks.tile([T, P, PARITIES], F32)
+                nc.vector.scalar_tensor_tensor(
+                    out=direct[:],
+                    in0=h[:, cols].rearrange("t (e p) -> t p e", e=PARITIES),
+                    scalar=SCALE,
+                    in1=cos_banks[b][:, cols].rearrange("t (p e) -> t p e", e=PARITIES),
+                    op0=MULT,
+                    op1=MULT,
+                )
+                directs.append(direct)
+            adder = nc.vector if b == N_BANKS - 1 else nc.gpsimd
+            for c in range(CHUNKS):
+                result = chunks.tile([T, P, PARITIES], F32)
+                adder.tensor_tensor(
+                    out=result[:],
+                    in0=directs[c][:],
+                    in1=crossed[:, :, c, :].rearrange("t e p -> t p e"),
+                    op=ADD,
+                )
+                first = b * BANK + c * CHUNK
+                nc.sync.dma_start(
+                    out=out_dram[:, first : first + CHUNK],
+                    in_=result[:].rearrange("t p e -> t (p e)"),
+                )

@@ -41,6 +41,14 @@ def group_words(copy, grouped, turned):
     copy(out=grouped.bitcast(F32), in_=turned[:].rearrange("p u r -> p r u"))
 
 
+def quantise(nc, grouped, codes, scales, dtype):
+    nc.vector.quantize_mx(
+        out=codes.bitcast(dtype),
+        scales=scales,
+        in_=grouped[:].rearrange("p r t -> p (r t)"),
+    )
+
+
 def tile_attention_pb_s_kernel(tc, Q, V, state, cos, sin, grad_out, out):
     nc = tc.nc
     v_dram = V.flatten_outer_dims()
@@ -51,7 +59,7 @@ def tile_attention_pb_s_kernel(tc, Q, V, state, cos, sin, grad_out, out):
         tc.tile_pool(name="keep", bufs=1) as keep,
         tc.tile_pool(name="banks", bufs=N_BANKS) as banks,
         tc.tile_pool(name="chunks", bufs=N_BANKS * CHUNKS) as chunks,
-        tc.tile_pool(name="planes", bufs=N_BANKS * CHUNKS * PARITIES) as planes,
+        tc.tile_pool(name="planes", bufs=N_BANKS * CHUNKS * PARITIES + 1) as planes,
         tc.psum_pool(name="psum_turn", bufs=TURN_BANKS) as psum_turn,
         tc.psum_pool(name="psum_h", bufs=N_BANKS) as psum_h,
         tc.manual_schedule(),
@@ -60,51 +68,49 @@ def tile_attention_pb_s_kernel(tc, Q, V, state, cos, sin, grad_out, out):
         make_identity(nc, ident[:])
 
         v_rows = keep.tile([T, D], BF16)
-        nc.sync.dma_start(out=v_rows[:], in_=v_dram)
         g_chunks = []
         for c in range(N_BANKS * CHUNKS):
             g_rows = chunks.tile([P, PARITIES, D], BF16)
-            nc.sync.dma_start(out=g_rows[:], in_=g_dram[c])
+            if c == 0:
+                nc.sync.dma_start(out=g_rows[:, 0, :], in_=g_dram[c][:, 0, :])
+                nc.sync.dma_start(out=v_rows[:], in_=v_dram)
+                nc.sync.dma_start(out=g_rows[:, 1, :], in_=g_dram[c][:, 1, :])
+            else:
+                nc.sync.dma_start(out=g_rows[:], in_=g_dram[c])
             g_chunks.append(g_rows)
-        sin_banks = []
-        cos_banks = []
-        for b in range(N_BANKS):
-            cols = slice(b * BANK, (b + 1) * BANK)
-            sin_sb = banks.tile([T, BANK], BF16)
-            nc.sync.dma_start(out=sin_sb[:], in_=sin[:, cols])
-            sin_banks.append(sin_sb)
-            cos_sb = banks.tile([T, BANK], BF16)
-            nc.sync.dma_start(out=cos_sb[:], in_=cos[:, cols])
-            cos_banks.append(cos_sb)
+        sin_sb = keep.tile([T, N], BF16)
+        nc.sync.dma_start(out=sin_sb[:], in_=sin)
+        cos_sb = keep.tile([T, N], BF16)
+        nc.sync.dma_start(out=cos_sb[:], in_=cos)
 
-        v_grouped = keep.tile([P, T, PACK], BF16, align_bytes=64)
         v_codes = keep.tile([P, T], U32, align_bytes=64)
         v_scales = keep.tile([P, T], U8, align_bytes=64)
-        v_turned = transpose_rows(nc, psum_turn, v_rows[:], ident[:])
-        group_words(nc.vector.tensor_copy, v_grouped[:], v_turned)
-        nc.vector.quantize_mx(
-            out=v_codes[:].bitcast(E4M3_X4),
-            scales=v_scales[:],
-            in_=v_grouped[:].rearrange("p r t -> p (r t)"),
-        )
-
         code_banks = []
         scale_banks = []
+        jobs = []
         for b in range(N_BANKS):
             g_codes = banks.tile([P, CHUNKS, PARITIES, P], U32, align_bytes=64)
             g_scales = banks.tile([P, CHUNKS, PARITIES, P], U8, align_bytes=64)
-            for c in range(CHUNKS):
-                for e in range(PARITIES):
-                    g_turned = transpose_rows(nc, psum_turn, g_chunks[b * CHUNKS + c][:, e, :], ident[:])
-                    g_grouped = planes.tile([P, P, PACK], BF16, align_bytes=64)
-                    group_words(nc.scalar.copy, g_grouped[:], g_turned)
-                    nc.vector.quantize_mx(
-                        out=g_codes[:, c, e, :].bitcast(E5M2_X4),
-                        scales=g_scales[:, c, e, :],
-                        in_=g_grouped[:].rearrange("p r t -> p (r t)"),
-                    )
             code_banks.append(g_codes)
             scale_banks.append(g_scales)
+            for c in range(CHUNKS):
+                for e in range(PARITIES):
+                    g_rows = g_chunks[b * CHUNKS + c]
+                    jobs.append((g_rows[:, e, :], g_codes[:, c, e, :], g_scales[:, c, e, :], E5M2_X4))
+        v_job = (v_rows[:], v_codes[:], v_scales[:], E4M3_X4)
+        last_job = jobs[-1]
+        jobs.insert(1, v_job)
+
+        waiting = []
+        for job in jobs:
+            rows, codes, scales, dtype = job
+            turned = transpose_rows(nc, psum_turn, rows, ident[:])
+            grouped = planes.tile([P, P, PACK], BF16, align_bytes=64)
+            group_words(nc.vector.tensor_copy if job is v_job or job is last_job else nc.scalar.copy, grouped[:], turned)
+            waiting.append((grouped, codes, scales, dtype))
+            if len(waiting) > 1:
+                quantise(nc, *waiting.pop(0))
+        quantise(nc, *waiting.pop(0))
 
         for b in range(N_BANKS):
             h = psum_h.tile([T, BANK], F32)
@@ -118,42 +124,39 @@ def tile_attention_pb_s_kernel(tc, Q, V, state, cos, sin, grad_out, out):
                 stop=True,
             )
 
-            crossed = banks.tile([T, PARITIES, CHUNKS, P], F32)
-            h_by_parity = h[:].rearrange("t (c e p) -> t e c p", c=CHUNKS, e=PARITIES)
-            sin_by_parity = sin_banks[b][:].rearrange("t (c p e) -> t e c p", c=CHUNKS, e=PARITIES)
-            for e in range(PARITIES):
-                partner = 1 - e
-                nc.vector.scalar_tensor_tensor(
-                    out=crossed[:, e, :, :],
-                    in0=h_by_parity[:, partner],
-                    scalar=SCALE if e == 0 else -SCALE,
-                    in1=sin_by_parity[:, partner],
-                    op0=MULT,
-                    op1=MULT,
-                )
-            directs = []
             for c in range(CHUNKS):
                 cols = slice(c * CHUNK, (c + 1) * CHUNK)
+                first = b * BANK + c * CHUNK
+                h_by_parity = h[:, cols].rearrange("t (e p) -> t e p", e=PARITIES)
+                sin_by_parity = sin_sb[:, first : first + CHUNK].rearrange("t (p e) -> t e p", e=PARITIES)
+                crossed = chunks.tile([T, PARITIES, P], F32)
+                for e in range(PARITIES):
+                    partner = 1 - e
+                    nc.vector.scalar_tensor_tensor(
+                        out=crossed[:, e, :],
+                        in0=h_by_parity[:, partner],
+                        scalar=SCALE if e == 0 else -SCALE,
+                        in1=sin_by_parity[:, partner],
+                        op0=MULT,
+                        op1=MULT,
+                    )
                 direct = chunks.tile([T, P, PARITIES], F32)
                 nc.vector.scalar_tensor_tensor(
                     out=direct[:],
                     in0=h[:, cols].rearrange("t (e p) -> t p e", e=PARITIES),
                     scalar=SCALE,
-                    in1=cos_banks[b][:, cols].rearrange("t (p e) -> t p e", e=PARITIES),
+                    in1=cos_sb[:, first : first + CHUNK].rearrange("t (p e) -> t p e", e=PARITIES),
                     op0=MULT,
                     op1=MULT,
                 )
-                directs.append(direct)
-            adder = nc.vector if b == N_BANKS - 1 else nc.gpsimd
-            for c in range(CHUNKS):
+                adder = nc.vector if first + CHUNK == N else nc.gpsimd
                 result = chunks.tile([T, P, PARITIES], F32)
                 adder.tensor_tensor(
                     out=result[:],
-                    in0=directs[c][:],
-                    in1=crossed[:, :, c, :].rearrange("t e p -> t p e"),
+                    in0=direct[:],
+                    in1=crossed[:].rearrange("t e p -> t p e"),
                     op=ADD,
                 )
-                first = b * BANK + c * CHUNK
                 nc.sync.dma_start(
                     out=out_dram[:, first : first + CHUNK],
                     in_=result[:].rearrange("t p e -> t (p e)"),

@@ -124,6 +124,7 @@ def tile_attention_pb_s_kernel(tc, Q, V, state, cos, sin, grad_out, out):
                 stop=True,
             )
 
+            products = []
             for c in range(CHUNKS):
                 cols = slice(c * CHUNK, (c + 1) * CHUNK)
                 first = b * BANK + c * CHUNK
@@ -149,7 +150,9 @@ def tile_attention_pb_s_kernel(tc, Q, V, state, cos, sin, grad_out, out):
                     op0=MULT,
                     op1=MULT,
                 )
-                adder = nc.vector if first + CHUNK == N else nc.gpsimd
+                products.append((first, direct, crossed))
+            adder = nc.vector if b == N_BANKS - 1 else nc.gpsimd
+            for first, direct, crossed in products:
                 result = chunks.tile([T, P, PARITIES], F32)
                 adder.tensor_tensor(
                     out=result[:],

@@ -25,6 +25,8 @@ N_BANKS = N // BANK
 CHUNKS = BANK // CHUNK
 TURN_BANKS = 8 - N_BANKS
 
+WARM = 384
+
 FLOPS = 2 * T * N * D
 BYTES = 2 * (T * D + N * D + 2 * T * N) + 4 * T * N
 
@@ -66,6 +68,11 @@ def tile_attention_pb_s_kernel(tc, Q, V, state, cos, sin, grad_out, out):
     ):
         ident = keep.tile([P, P], F32)
         make_identity(nc, ident[:])
+
+        zeros = keep.tile([P, WARM], F32)
+        nc.vector.memset(zeros[:], 0.0)
+        warm = psum_h.tile([P, WARM], F32, tag="h")
+        nc.tensor.matmul(warm[:], lhsT=zeros[:, :P], rhs=zeros[:], start=True, stop=True)
 
         v_rows = keep.tile([T, D], BF16)
         g_chunks = []

@@ -23,7 +23,9 @@ CHUNK = P * PARITIES
 BANK = 512
 N_BANKS = N // BANK
 CHUNKS = BANK // CHUNK
-TURN_BANKS = 8 - N_BANKS
+N_PLANES = N // P
+N_H = 2
+TURN_BANKS = 8 - N_H
 
 WARM = 384
 
@@ -63,16 +65,18 @@ def tile_attention_pb_s_kernel(tc, Q, V, state, cos, sin, grad_out, out):
         tc.tile_pool(name="chunks", bufs=N_BANKS * CHUNKS) as chunks,
         tc.tile_pool(name="planes", bufs=N_BANKS * CHUNKS * PARITIES + 1) as planes,
         tc.psum_pool(name="psum_turn", bufs=TURN_BANKS) as psum_turn,
-        tc.psum_pool(name="psum_h", bufs=N_BANKS) as psum_h,
+        tc.psum_pool(name="psum_h", bufs=N_H) as psum_h,
         tc.manual_schedule(),
     ):
         ident = keep.tile([P, P], F32)
         make_identity(nc, ident[:])
 
-        zeros = keep.tile([P, WARM], F32)
+        zeros = keep.tile([P, P], F32)
         nc.vector.memset(zeros[:], 0.0)
         warm = psum_h.tile([P, WARM], F32, tag="h")
-        nc.tensor.matmul(warm[:], lhsT=zeros[:, :P], rhs=zeros[:], start=True, stop=True)
+        nc.tensor.matmul(
+            warm[:], lhsT=zeros[:], rhs=zeros[:, :1].to_broadcast([P, WARM]), start=True, stop=True
+        )
 
         v_rows = keep.tile([T, D], BF16)
         g_chunks = []
@@ -92,82 +96,105 @@ def tile_attention_pb_s_kernel(tc, Q, V, state, cos, sin, grad_out, out):
 
         v_codes = keep.tile([P, T], U32, align_bytes=64)
         v_scales = keep.tile([P, T], U8, align_bytes=64)
-        code_banks = []
-        scale_banks = []
-        jobs = []
-        for b in range(N_BANKS):
-            g_codes = banks.tile([P, CHUNKS, PARITIES, P], U32, align_bytes=64)
-            g_scales = banks.tile([P, CHUNKS, PARITIES, P], U8, align_bytes=64)
-            code_banks.append(g_codes)
-            scale_banks.append(g_scales)
-            for c in range(CHUNKS):
-                for e in range(PARITIES):
-                    g_rows = g_chunks[b * CHUNKS + c]
-                    jobs.append((g_rows[:, e, :], g_codes[:, c, e, :], g_scales[:, c, e, :], E5M2_X4))
-        v_job = (v_rows[:], v_codes[:], v_scales[:], E4M3_X4)
-        last_job = jobs[-1]
-        jobs.insert(1, v_job)
+        g_codes = keep.tile([P, N], U32, align_bytes=64)
+        g_scales = keep.tile([P, N], U8, align_bytes=64)
 
-        waiting = []
-        for job in jobs:
-            rows, codes, scales, dtype = job
+        def turn(rows, copy):
             turned = transpose_rows(nc, psum_turn, rows, ident[:])
             grouped = planes.tile([P, P, PACK], BF16, align_bytes=64)
-            group_words(nc.vector.tensor_copy if job is v_job or job is last_job else nc.scalar.copy, grouped[:], turned)
-            waiting.append((grouped, codes, scales, dtype))
-            if len(waiting) > 1:
-                quantise(nc, *waiting.pop(0))
-        quantise(nc, *waiting.pop(0))
+            group_words(copy, grouped[:], turned)
+            return grouped
 
-        for b in range(N_BANKS):
+        def quantise_plane(i, grouped):
+            cols = slice(i * P, (i + 1) * P)
+            quantise(nc, grouped, g_codes[:, cols], g_scales[:, cols], E5M2_X4)
+
+        def multiply(first):
             h = psum_h.tile([T, BANK], F32)
+            cols = slice(first, first + BANK)
             nc.tensor.matmul_mx(
                 out=h[:],
                 lhsT=v_codes[:].bitcast(E4M3_X4),
                 lhsT_scale=v_scales[:],
-                rhs=code_banks[b][:].rearrange("p c e r -> p (c e r)").bitcast(E5M2_X4),
-                rhs_scale=scale_banks[b][:].rearrange("p c e r -> p (c e r)"),
+                rhs=g_codes[:, cols].bitcast(E5M2_X4),
+                rhs_scale=g_scales[:, cols],
                 start=True,
                 stop=True,
             )
+            return h
 
-            products = []
-            for c in range(CHUNKS):
-                cols = slice(c * CHUNK, (c + 1) * CHUNK)
-                first = b * BANK + c * CHUNK
-                h_by_parity = h[:, cols].rearrange("t (e p) -> t e p", e=PARITIES)
-                sin_by_parity = sin_sb[:, first : first + CHUNK].rearrange("t (p e) -> t e p", e=PARITIES)
-                crossed = chunks.tile([T, PARITIES, P], F32)
-                for e in range(PARITIES):
-                    partner = 1 - e
-                    nc.vector.scalar_tensor_tensor(
-                        out=crossed[:, e, :],
-                        in0=h_by_parity[:, partner],
-                        scalar=SCALE if e == 0 else -SCALE,
-                        in1=sin_by_parity[:, partner],
-                        op0=MULT,
-                        op1=MULT,
-                    )
-                direct = chunks.tile([T, P, PARITIES], F32)
+        def crossed_product(c, h_chunk):
+            first = c * CHUNK
+            h_by_parity = h_chunk.rearrange("t (e p) -> t e p", e=PARITIES)
+            sin_by_parity = sin_sb[:, first : first + CHUNK].rearrange("t (p e) -> t e p", e=PARITIES)
+            crossed = chunks.tile([T, PARITIES, P], F32)
+            for e in range(PARITIES):
+                partner = 1 - e
                 nc.vector.scalar_tensor_tensor(
-                    out=direct[:],
-                    in0=h[:, cols].rearrange("t (e p) -> t p e", e=PARITIES),
-                    scalar=SCALE,
-                    in1=cos_sb[:, first : first + CHUNK].rearrange("t (p e) -> t p e", e=PARITIES),
+                    out=crossed[:, e, :],
+                    in0=h_by_parity[:, partner],
+                    scalar=SCALE if e == 0 else -SCALE,
+                    in1=sin_by_parity[:, partner],
                     op0=MULT,
                     op1=MULT,
                 )
-                products.append((first, direct, crossed))
-            adder = nc.vector if b == N_BANKS - 1 else nc.gpsimd
-            for first, direct, crossed in products:
-                result = chunks.tile([T, P, PARITIES], F32)
-                adder.tensor_tensor(
-                    out=result[:],
-                    in0=direct[:],
-                    in1=crossed[:].rearrange("t e p -> t p e"),
-                    op=ADD,
-                )
-                nc.sync.dma_start(
-                    out=out_dram[:, first : first + CHUNK],
-                    in_=result[:].rearrange("t p e -> t (p e)"),
-                )
+            return crossed
+
+        def direct_product(c, h_chunk):
+            first = c * CHUNK
+            direct = chunks.tile([T, P, PARITIES], F32)
+            nc.vector.scalar_tensor_tensor(
+                out=direct[:],
+                in0=h_chunk.rearrange("t (e p) -> t p e", e=PARITIES),
+                scalar=SCALE,
+                in1=cos_sb[:, first : first + CHUNK].rearrange("t (p e) -> t p e", e=PARITIES),
+                op0=MULT,
+                op1=MULT,
+            )
+            return direct
+
+        def add_and_store(adder, c, crossed, direct):
+            first = c * CHUNK
+            result = chunks.tile([T, P, PARITIES], F32)
+            adder.tensor_tensor(
+                out=result[:],
+                in0=direct[:],
+                in1=crossed[:].rearrange("t e p -> t p e"),
+                op=ADD,
+            )
+            nc.sync.dma_start(
+                out=out_dram[:, first : first + CHUNK],
+                in_=result[:].rearrange("t p e -> t (p e)"),
+            )
+
+        def rows_of(i):
+            return g_chunks[i // PARITIES][:, i % PARITIES, :]
+
+        planes_of = []
+        for i in range(N_PLANES):
+            planes_of.append(turn(rows_of(i), nc.vector.tensor_copy if i == 2 else nc.scalar.copy))
+            if i == 0:
+                v_grouped = turn(v_rows[:], nc.vector.tensor_copy)
+            else:
+                quantise_plane(i - 1, planes_of[i - 1])
+            if i == 1:
+                quantise(nc, v_grouped, v_codes[:], v_scales[:], E4M3_X4)
+        h01 = multiply(0)
+        h0 = h01[:, :CHUNK]
+        h1 = h01[:, CHUNK:]
+        quantise_plane(N_PLANES - 1, planes_of[N_PLANES - 1])
+        x0 = crossed_product(0, h0)
+        h23 = multiply(BANK)
+        d0 = direct_product(0, h0)
+        add_and_store(nc.gpsimd, 0, x0, d0)
+        x1 = crossed_product(1, h1)
+        d1 = direct_product(1, h1)
+        add_and_store(nc.gpsimd, 1, x1, d1)
+        h2 = h23[:, :CHUNK]
+        h3 = h23[:, CHUNK:]
+        x2 = crossed_product(2, h2)
+        d2 = direct_product(2, h2)
+        x3 = crossed_product(3, h3)
+        d3 = direct_product(3, h3)
+        add_and_store(nc.vector, 2, x2, d2)
+        add_and_store(nc.vector, 3, x3, d3)

@@ -90,9 +90,11 @@ def tile_attention_pb_s_kernel(tc, Q, V, state, cos, sin, grad_out, out):
                 nc.sync.dma_start(out=g_rows[:], in_=g_dram[c])
             g_chunks.append(g_rows)
         sin_sb = keep.tile([T, N], BF16)
-        nc.sync.dma_start(out=sin_sb[:], in_=sin)
         cos_sb = keep.tile([T, N], BF16)
-        nc.sync.dma_start(out=cos_sb[:], in_=cos)
+        for b in range(N_BANKS):
+            cols = slice(b * BANK, (b + 1) * BANK)
+            nc.sync.dma_start(out=sin_sb[:, cols], in_=sin[:, cols])
+            nc.sync.dma_start(out=cos_sb[:, cols], in_=cos[:, cols])
 
         v_codes = keep.tile([P, T], U32, align_bytes=64)
         v_scales = keep.tile([P, T], U8, align_bytes=64)

@@ -86,6 +86,9 @@ def tile_attention_pb_s_kernel(tc, Q, V, state, cos, sin, grad_out, out):
                 nc.sync.dma_start(out=g_rows[:, 0, :], in_=g_dram[c][:, 0, :])
                 nc.sync.dma_start(out=v_rows[:], in_=v_dram)
                 nc.sync.dma_start(out=g_rows[:, 1, :], in_=g_dram[c][:, 1, :])
+            elif c == N // CHUNK - 1:
+                for e in range(PARITIES):
+                    nc.sync.dma_start(out=g_rows[:, e, :], in_=g_dram[c][:, e, :])
             else:
                 nc.sync.dma_start(out=g_rows[:], in_=g_dram[c])
             g_chunks.append(g_rows)
@@ -155,7 +158,7 @@ def tile_attention_pb_s_kernel(tc, Q, V, state, cos, sin, grad_out, out):
             )
             return direct
 
-        def add_and_store(adder, c, crossed, direct):
+        def add_and_store(adder, queue, c, crossed, direct):
             first = c * CHUNK
             result = chunks.tile([T, P, PARITIES], F32)
             adder.tensor_tensor(
@@ -164,7 +167,7 @@ def tile_attention_pb_s_kernel(tc, Q, V, state, cos, sin, grad_out, out):
                 in1=crossed[:].rearrange("t e p -> t p e"),
                 op=ADD,
             )
-            nc.sync.dma_start(
+            queue.dma_start(
                 out=out_dram[:, first : first + CHUNK],
                 in_=result[:].rearrange("t p e -> t (p e)"),
             )
@@ -188,15 +191,15 @@ def tile_attention_pb_s_kernel(tc, Q, V, state, cos, sin, grad_out, out):
         x0 = crossed_product(0, h0)
         h23 = multiply(BANK)
         d0 = direct_product(0, h0)
-        add_and_store(nc.gpsimd, 0, x0, d0)
+        add_and_store(nc.gpsimd, nc.scalar, 0, x0, d0)
         x1 = crossed_product(1, h1)
         d1 = direct_product(1, h1)
-        add_and_store(nc.gpsimd, 1, x1, d1)
+        add_and_store(nc.gpsimd, nc.scalar, 1, x1, d1)
         h2 = h23[:, :CHUNK]
         h3 = h23[:, CHUNK:]
         x2 = crossed_product(2, h2)
         d2 = direct_product(2, h2)
         x3 = crossed_product(3, h3)
         d3 = direct_product(3, h3)
-        add_and_store(nc.vector, 2, x2, d2)
-        add_and_store(nc.vector, 3, x3, d3)
+        add_and_store(nc.vector, nc.sync, 2, x2, d2)
+        add_and_store(nc.vector, nc.sync, 3, x3, d3)

@@ -27,8 +27,6 @@ N_PLANES = N // P
 N_H = 2
 TURN_BANKS = 8 - N_H
 
-WARM = 384
-
 FLOPS = 2 * T * N * D
 BYTES = 2 * (T * D + N * D + 2 * T * N) + 4 * T * N
 
@@ -70,13 +68,6 @@ def tile_attention_pb_s_kernel(tc, Q, V, state, cos, sin, grad_out, out):
     ):
         ident = keep.tile([P, P], F32)
         make_identity(nc, ident[:])
-
-        zeros = keep.tile([P, P], F32)
-        nc.vector.memset(zeros[:], 0.0)
-        warm = psum_h.tile([P, WARM], F32, tag="h")
-        nc.tensor.matmul(
-            warm[:], lhsT=zeros[:], rhs=zeros[:, :1].to_broadcast([P, WARM]), start=True, stop=True
-        )
 
         v_rows = keep.tile([T, D], BF16)
         g_chunks = []

import concourse.mybir as mybir
from concourse.masks import make_identity

F32 = mybir.dt.float32
BF16 = mybir.dt.bfloat16
U32 = mybir.dt.uint32
U8 = mybir.dt.uint8
E4M3_X4 = mybir.dt.float8_e4m3fn_x4
E5M2_X4 = mybir.dt.float8_e5m2_x4
MULT = mybir.AluOpType.mult
ADD = mybir.AluOpType.add

P = 128
PACK = 4
T = 128
D = 512
N = 1024
SCALE = N ** -0.5

HALVES = D // 2 // P
PARITIES = 2
CHUNK = P * PARITIES
BANK = 512
N_BANKS = N // BANK
CHUNKS = BANK // CHUNK
N_PLANES = N // P
N_H = 2
TURN_BANKS = 8 - N_H

FLOPS = 2 * T * N * D
BYTES = 2 * (T * D + N * D + 2 * T * N) + 4 * T * N


def transpose_rows(nc, psum, rows, ident):
    words = rows.bitcast(F32)
    turned = psum.tile([P, HALVES, P], F32, tag="turned")
    for u in range(HALVES):
        nc.tensor.transpose(turned[:, u, :], words[:, u :: HALVES], ident)
    return turned


def group_words(copy, grouped, turned):
    copy(out=grouped.bitcast(F32), in_=turned[:].rearrange("p u r -> p r u"))


def quantise(nc, grouped, codes, scales, dtype):
    nc.vector.quantize_mx(
        out=codes.bitcast(dtype),
        scales=scales,
        in_=grouped[:].rearrange("p r t -> p (r t)"),
    )


def tile_attention_pb_s_kernel(tc, Q, V, state, cos, sin, grad_out, out):
    nc = tc.nc
    v_dram = V.flatten_outer_dims()
    out_dram = out.flatten_outer_dims()
    g_dram = grad_out.flatten_outer_dims().rearrange("(c p e) d -> c p e d", p=P, e=PARITIES)

    with (
        tc.tile_pool(name="keep", bufs=1) as keep,
        tc.tile_pool(name="banks", bufs=N_BANKS) as banks,
        tc.tile_pool(name="chunks", bufs=N_BANKS * CHUNKS) as chunks,
        tc.tile_pool(name="planes", bufs=N_BANKS * CHUNKS * PARITIES + 1) as planes,
        tc.psum_pool(name="psum_turn", bufs=TURN_BANKS) as psum_turn,
        tc.psum_pool(name="psum_h", bufs=N_H) as psum_h,
        tc.manual_schedule(),
    ):
        ident = keep.tile([P, P], F32)
        make_identity(nc, ident[:])

        v_rows = keep.tile([T, D], BF16)
        g_chunks = []
        for c in range(N_BANKS * CHUNKS):
            g_rows = chunks.tile([P, PARITIES, D], BF16)
            if c == 0:
                nc.sync.dma_start(out=g_rows[:, 0, :], in_=g_dram[c][:, 0, :])
                nc.sync.dma_start(out=v_rows[:], in_=v_dram)
                nc.sync.dma_start(out=g_rows[:, 1, :], in_=g_dram[c][:, 1, :])
            elif c == N // CHUNK - 1:
                for e in range(PARITIES):
                    nc.sync.dma_start(out=g_rows[:, e, :], in_=g_dram[c][:, e, :])
            else:
                nc.sync.dma_start(out=g_rows[:], in_=g_dram[c])
            g_chunks.append(g_rows)
        sin_sb = keep.tile([T, N], BF16)
        cos_sb = keep.tile([T, N], BF16)
        for b in range(N_BANKS):
            cols = slice(b * BANK, (b + 1) * BANK)
            nc.sync.dma_start(out=sin_sb[:, cols], in_=sin[:, cols])
            nc.sync.dma_start(out=cos_sb[:, cols], in_=cos[:, cols])

        v_codes = keep.tile([P, T], U32, align_bytes=64)
        v_scales = keep.tile([P, T], U8, align_bytes=64)
        g_codes = keep.tile([P, N], U32, align_bytes=64)
        g_scales = keep.tile([P, N], U8, align_bytes=64)

        def turn(rows, copy):
            turned = transpose_rows(nc, psum_turn, rows, ident[:])
            grouped = planes.tile([P, P, PACK], BF16, align_bytes=64)
            group_words(copy, grouped[:], turned)
            return grouped

        def quantise_plane(i, grouped):
            cols = slice(i * P, (i + 1) * P)
            quantise(nc, grouped, g_codes[:, cols], g_scales[:, cols], E5M2_X4)

        def multiply(first):
            h = psum_h.tile([T, BANK], F32)
            cols = slice(first, first + BANK)
            nc.tensor.matmul_mx(
                out=h[:],
                lhsT=v_codes[:].bitcast(E4M3_X4),
                lhsT_scale=v_scales[:],
                rhs=g_codes[:, cols].bitcast(E5M2_X4),
                rhs_scale=g_scales[:, cols],
                start=True,
                stop=True,
            )
            return h

        def crossed_product(c, h_chunk):
            first = c * CHUNK
            h_by_parity = h_chunk.rearrange("t (e p) -> t e p", e=PARITIES)
            sin_by_parity = sin_sb[:, first : first + CHUNK].rearrange("t (p e) -> t e p", e=PARITIES)
            crossed = chunks.tile([T, PARITIES, P], F32)
            for e in range(PARITIES):
                partner = 1 - e
                nc.vector.scalar_tensor_tensor(
                    out=crossed[:, e, :],
                    in0=h_by_parity[:, partner],
                    scalar=SCALE if e == 0 else -SCALE,
                    in1=sin_by_parity[:, partner],
                    op0=MULT,
                    op1=MULT,
                )
            return crossed

        def direct_product(c, h_chunk):
            first = c * CHUNK
            direct = chunks.tile([T, P, PARITIES], F32)
            nc.vector.scalar_tensor_tensor(
                out=direct[:],
                in0=h_chunk.rearrange("t (e p) -> t p e", e=PARITIES),
                scalar=SCALE,
                in1=cos_sb[:, first : first + CHUNK].rearrange("t (p e) -> t p e", e=PARITIES),
                op0=MULT,
                op1=MULT,
            )
            return direct

        def add_and_store(adder, queue, c, crossed, direct):
            first = c * CHUNK
            result = chunks.tile([T, P, PARITIES], F32)
            adder.tensor_tensor(
                out=result[:],
                in0=direct[:],
                in1=crossed[:].rearrange("t e p -> t p e"),
                op=ADD,
            )
            queue.dma_start(
                out=out_dram[:, first : first + CHUNK],
                in_=result[:].rearrange("t p e -> t (p e)"),
            )

        def rows_of(i):
            return g_chunks[i // PARITIES][:, i % PARITIES, :]

        planes_of = []
        for i in range(N_PLANES):
            planes_of.append(turn(rows_of(i), nc.vector.tensor_copy if i == 2 else nc.scalar.copy))
            if i == 0:
                v_grouped = turn(v_rows[:], nc.vector.tensor_copy)
            else:
                quantise_plane(i - 1, planes_of[i - 1])
            if i == 1:
                quantise(nc, v_grouped, v_codes[:], v_scales[:], E4M3_X4)
        h01 = multiply(0)
        h0 = h01[:, :CHUNK]
        h1 = h01[:, CHUNK:]
        quantise_plane(N_PLANES - 1, planes_of[N_PLANES - 1])
        x0 = crossed_product(0, h0)
        h23 = multiply(BANK)
        d0 = direct_product(0, h0)
        add_and_store(nc.gpsimd, nc.scalar, 0, x0, d0)
        x1 = crossed_product(1, h1)
        d1 = direct_product(1, h1)
        add_and_store(nc.gpsimd, nc.scalar, 1, x1, d1)
        h2 = h23[:, :CHUNK]
        h3 = h23[:, CHUNK:]
        x2 = crossed_product(2, h2)
        d2 = direct_product(2, h2)
        x3 = crossed_product(3, h3)
        d3 = direct_product(3, h3)
        add_and_store(nc.vector, nc.sync, 2, x2, d2)
        add_and_store(nc.vector, nc.sync, 3, x3, d3)
